import numpy as np
import ml_dtypes


def mxq(x, axis, fmt="e4m3"):
    dtype, down = {"e4m3": (ml_dtypes.float8_e4m3fn, 7), "e5m2": (ml_dtypes.float8_e5m2, 14)}[fmt]
    v = np.moveaxis(np.asarray(x, np.float32).astype(ml_dtypes.bfloat16).astype(np.float64), axis, -1)
    blocks = v.reshape(v.shape[:-1] + (-1, 32))
    amax = np.abs(blocks).max(-1, keepdims=True)
    byte = np.maximum(np.where(amax > 0, np.frexp(amax)[1] - 1 + 127, 0) - down, 1)
    scale = np.exp2(byte - 127.0)
    codes = (blocks / scale).astype(np.float32).astype(dtype).astype(np.float64)
    return np.moveaxis((codes * scale).reshape(v.shape), -1, axis)


WIDE = False


def mx_kscale(k):
    if not WIDE:
        return np.ones(k)
    levels = np.array([10, -10, 5, -5, 0])
    a = np.random.permutation(np.resize(levels, k // 512 * 4)).reshape(k // 512, 4)
    idx = np.arange(k)
    return np.exp2(a[idx // 512, idx % 128 // 32])


BF16 = ml_dtypes.bfloat16


def bf(x):
    return np.asarray(x, np.float32).astype(BF16)


def f64(x):
    return np.asarray(x).astype(np.float64)


B, T, D, H, HD, FF = 4, 1024, 1024, 4, 128, 256
EPS = 1.1920928955078125e-07
DA = H * HD


def rmsnorm(x, w):
    ms = np.mean(np.square(x), axis=-1, keepdims=True)
    return x * (1.0 / np.sqrt(ms + EPS)) * w


def silu(v):
    return v / (1.0 + np.exp(-v))


def setup_inputs():
    s = mx_kscale(DA)
    t = mx_kscale(D)
    return {
        "attn_out": bf(np.random.standard_normal((B, T, DA)) * 0.3 * s),
        "x": bf(np.random.standard_normal((B, T, D))),
        "o_w": bf(np.random.standard_normal((D, DA)) * 1.5 / np.sqrt(DA) / s[None, :]),
        "norm2_w": bf(1.0 + 0.1 * np.random.standard_normal(D)),
        "scale_gamma": bf(np.random.uniform(0.5, 1.5, D) * t),
        "scale_beta": bf(np.random.standard_normal(D) * 0.2 * t),
        "gate_w": bf(np.random.standard_normal((FF, D)) / np.sqrt(D) / t[None, :]),
        "up_w": bf(np.random.standard_normal((FF, D)) / np.sqrt(D) / t[None, :]),
    }


def reference(attn_out, x, o_w, norm2_w, scale_gamma, scale_beta, gate_w, up_w):
    x1 = f64(x) + (mxq(f64(attn_out), 2, "e4m3") @ mxq(f64(o_w), 1, "e4m3").T)
    h = rmsnorm(x1, f64(norm2_w)) * f64(scale_gamma) + f64(scale_beta)
    hq = mxq(h, 2, "e4m3")
    ff = silu(hq @ mxq(f64(gate_w), 1, "e4m3").T) * (hq @ mxq(f64(up_w), 1, "e4m3").T)
    return x1, ff

@@ -1,0 +1,327 @@
+from contextlib import ExitStack
+
+import concourse.mybir as mybir
+from concourse.masks import make_identity
+
+F32 = mybir.dt.float32
+BF16 = mybir.dt.bfloat16
+U32 = mybir.dt.uint32
+U8 = mybir.dt.uint8
+FP8X4 = mybir.dt.float8_e4m3fn_x4
+ALU = mybir.AluOpType
+ACT = mybir.ActivationFunctionType
+
+P = 128
+NTOK = 4096
+DA = 512
+D = 1024
+FF = 256
+NT = NTOK // P
+NG = NT // 4
+FLOPS = 2 * NTOK * DA * D + 2 * NTOK * D * 2 * FF
+
+MANUAL = False
+LY = 6
+LS = LY + 5
+XB = 5
+P4_ON_V = ()
+ATCOPY_V = True
+
+
+def tile_fractalblock_pb_t_kernel(tc, attn_out, x, o_w, norm2_w, scale_gamma, scale_beta, gate_w, up_w, out_0, out_1):
+    nc = tc.nc
+    attn_f = attn_out.flatten_outer_dims()
+    x_f = x.flatten_outer_dims()
+    o0_f = out_0.flatten_outer_dims()
+    o1_f = out_1.flatten_outer_dims()
+
+    with ExitStack() as ctx:
+        const = ctx.enter_context(tc.tile_pool(name="const", bufs=1))
+        io = ctx.enter_context(tc.tile_pool(name="io", bufs=XB))
+        work = ctx.enter_context(tc.tile_pool(name="work", bufs=2))
+        small = ctx.enter_context(tc.tile_pool(name="small", bufs=8))
+        psum = ctx.enter_context(tc.psum_pool(name="psum", bufs=2))
+        if MANUAL:
+            ctx.enter_context(tc.manual_schedule())
+
+        ident_f = const.tile([P, P], F32, name="ident_f")
+        make_identity(nc, ident_f[:])
+        ident_b = const.tile([P, P], BF16, name="ident_b")
+        make_identity(nc, ident_b[:])
+        neg_half = const.tile([P, 1], F32, name="neg_half")
+        nc.vector.memset(neg_half[:], -0.5)
+        vec = const.tile([P, P], BF16, name="vec")
+        nc.vector.memset(vec[:], 0.0)
+        vcol = const.tile([P, 24], F32, name="vcol")
+        g32 = const.tile([P, 8], F32, name="g32")
+        ow_codes = const.tile([P, D], U32, name="ow_codes", align_bytes=64)
+        ow_scales = const.tile([P, D], U8, name="ow_scales", align_bytes=64)
+        w_codes = const.tile([P, 2, 512], U32, name="w_codes", align_bytes=64)
+        w_scales = const.tile([P, 2, 512], U8, name="w_scales", align_bytes=64)
+
+        x_sb = {}
+        at_sb = {}
+
+        def load(g):
+            a = io.tile([P, 4 * DA], BF16, name="at_sb", tag="at_sb")
+            nc.sync.dma_start(out=a[:], in_=attn_f[g * 512:(g + 1) * 512, :].rearrange("(p j) k -> p (j k)", j=4))
+            at_sb[g] = a
+            xx = io.tile([P, 4, D], BF16, name="x_sb", tag="x_sb")
+            nc.sync.dma_start(out=xx[:], in_=x_f[g * 512:(g + 1) * 512, :].rearrange("(p j) d -> p j d", j=4))
+            x_sb[g] = xx
+
+        a0 = io.tile([P, 4 * DA], BF16, name="at_sb", tag="at_sb")
+        nc.sync.dma_start(out=a0[:], in_=attn_f[0:512, :].rearrange("(p j) k -> p (j k)", j=4))
+        at_sb[0] = a0
+        ow_sb = work.tile([P, 8, DA], BF16, name="ow_sb", tag="H")
+        nc.sync.dma_start(out=ow_sb[:], in_=o_w.rearrange("(t p) k -> p t k", p=P))
+        x0 = io.tile([P, 4, D], BF16, name="x_sb", tag="x_sb")
+        nc.sync.dma_start(out=x0[:], in_=x_f[0:512, :].rearrange("(p j) d -> p j d", j=4))
+        x_sb[0] = x0
+        nc.scalar.dma_start(out=vec[0:8, :], in_=norm2_w.rearrange("(c p) -> c p", p=P))
+        nc.scalar.dma_start(out=vec[8:16, :], in_=scale_gamma.rearrange("(c p) -> c p", p=P))
+        nc.scalar.dma_start(out=vec[16:24, :], in_=scale_beta.rearrange("(c p) -> c p", p=P))
+        w_sb = work.tile([P, 4, D], BF16, name="w_sb", tag="H")
+        nc.sync.dma_start(out=w_sb[:, 0:2, :], in_=gate_w.rearrange("(r p) k -> p r k", p=P))
+        nc.sync.dma_start(out=w_sb[:, 2:4, :], in_=up_w.rearrange("(r p) k -> p r k", p=P))
+        for g in range(1, XB):
+            load(g)
+
+        owg = work.tile([P, 4 * D], BF16, name="owg", tag="hg", align_bytes=64)
+        owg_f = owg[:].bitcast(F32)
+        ow_f = ow_sb[:].rearrange("p t k -> p (t k)").bitcast(F32)
+        for b in range(4):
+            ps = psum.tile([P, 2, 2, P], F32, name="ow_ps", tag="tp", bufs=3)
+            for tt in range(2):
+                for u in range(2):
+                    c0 = (2 * b + tt) * 256 + u * P
+                    nc.tensor.transpose(ps[:, tt, u, :], ow_f[:, c0:c0 + P], ident_f[:])
+            dst = owg_f[:, b * 512:(b + 1) * 512].rearrange("p (t m u) -> p t m u", t=2, u=2)
+            src = ps[:].rearrange("p t u m -> p t m u")
+            if b % 2 == 0:
+                nc.vector.tensor_copy(out=dst, in_=src)
+            else:
+                nc.scalar.copy(out=dst, in_=src)
+            if b % 2 == 1:
+                h = b // 2
+                nc.vector.quantize_mx(
+                    out=ow_codes[:, h * 512:(h + 1) * 512].bitcast(FP8X4),
+                    scales=ow_scales[:, h * 512:(h + 1) * 512],
+                    in_=owg[:, h * 2048:(h + 1) * 2048],
+                )
+
+        a_codes = {}
+        a_scales = {}
+
+        def attn_t(q):
+            g, pi = divmod(q, 2)
+            af = at_sb[g][:].bitcast(F32)
+            ps = psum.tile([P, 2, 2, P], F32, name="at_ps", tag="tp", bufs=3)
+            for jj in range(2):
+                for u in range(2):
+                    c0 = (2 * pi + jj) * 256 + u * P
+                    nc.tensor.transpose(ps[:, jj, u, :], af[:, c0:c0 + P], ident_f[:])
+            ag = work.tile([P, 1024], BF16, name="ag", tag="ag", bufs=3, align_bytes=64)
+            dst = ag[:].bitcast(F32).rearrange("p (t m u) -> p t m u", t=2, u=2)
+            src = ps[:].rearrange("p t u m -> p t m u")
+            if ATCOPY_V:
+                nc.vector.tensor_copy(out=dst, in_=src)
+            else:
+                nc.scalar.copy(out=dst, in_=src)
+            return ag
+
+        def attn_q(q, ag):
+            ac = work.tile([P, 256], U32, name="ac", tag="ac", bufs=4, align_bytes=64)
+            asc = work.tile([P, 256], U8, name="asc", tag="asc", bufs=4, align_bytes=64)
+            nc.vector.quantize_mx(out=ac[:].bitcast(FP8X4), scales=asc[:], in_=ag[:])
+            a_codes[q] = ac
+            a_scales[q] = asc
+
+        x1_t = {}
+        y_t = {}
+
+        def s1_mm(n):
+            q, jj = divmod(n, 2)
+            outs = []
+            for hf in range(2):
+                ps = psum.tile([P, 512], F32, name="s1_ps", tag="s1", bufs=3)
+                nc.tensor.matmul_mx(
+                    out=ps[:],
+                    lhsT=a_codes[q][:, jj * P:(jj + 1) * P].bitcast(FP8X4),
+                    lhsT_scale=a_scales[q][:, jj * P:(jj + 1) * P],
+                    rhs=ow_codes[:, hf * 512:(hf + 1) * 512].bitcast(FP8X4),
+                    rhs_scale=ow_scales[:, hf * 512:(hf + 1) * 512],
+                    start=True,
+                    stop=True,
+                )
+                outs.append(ps)
+            return outs
+
+        def p1(n, pss):
+            q, jj = divmod(n, 2)
+            g, j = divmod(n, 4)
+            if jj == 0:
+                x1_t[q] = work.tile([P, 2, D], F32, name="x1", tag="x1", bufs=4)
+            for hf in range(2):
+                nc.vector.tensor_tensor(
+                    out=x1_t[q][:, jj, hf * 512:(hf + 1) * 512],
+                    in0=pss[hf][:],
+                    in1=x_sb[g][:, j, hf * 512:(hf + 1) * 512],
+                    op=ALU.add,
+                )
+            if jj == 1:
+                pi = q % 2
+                nc.sync.dma_start(
+                    out=o0_f[g * 512:(g + 1) * 512, :].rearrange("(p j) d -> p j d", j=4)[:, 2 * pi:2 * pi + 2, :],
+                    in_=x1_t[q][:],
+                )
+
+        def norm(n):
+            q, jj = divmod(n, 2)
+            junk = work.tile([P, D], BF16, name="junk", tag="junk", bufs=2)
+            ss = small.tile([P, 1], F32, name="ss", tag="ss")
+            nc.scalar.activation(out=junk[:], in_=x1_t[q][:, jj, :], func=ACT.Square, accum_out=ss[:])
+            sse = small.tile([P, 1], F32, name="sse", tag="sse")
+            nc.gpsimd.tensor_scalar(out=sse[:], in0=ss[:], scalar1=1.0, scalar2=2.0 ** -13, op0=ALU.mult, op1=ALU.add)
+            r = small.tile([P, 1], F32, name="r", tag="r")
+            nc.gpsimd.tensor_tensor(out=r[:], in0=sse[:], in1=neg_half[:], op=ALU.pow)
+            y = work.tile([P, D], F32, name="y", tag="y", bufs=12)
+            nc.gpsimd.tensor_scalar(out=y[:], in0=x1_t[q][:, jj, :], scalar1=r[:, 0:1], scalar2=0.0, op0=ALU.mult, op1=ALU.add)
+            y_t[n] = y
+
+        H_t = {}
+        hg_t = {}
+        h_codes = {}
+        h_scales = {}
+
+        def yt(g, c8):
+            if c8 == 0:
+                H_t[g] = work.tile([P, 8, 512], BF16, name="H", tag="H")
+            ps = psum.tile([P, 4, P], F32, name="yt_ps", tag="tp", bufs=3)
+            for j in range(4):
+                nc.tensor.transpose(ps[:, j, :], y_t[4 * g + j][:, c8 * P:(c8 + 1) * P], ident_f[:])
+            return ps
+
+        def p4(g, c8, ps):
+            src = ps[:].rearrange("p j m -> p (j m)")
+            if c8 in P4_ON_V:
+                nc.vector.tensor_scalar(
+                    out=H_t[g][:, c8, :], in0=src, scalar1=g32[:, c8:c8 + 1], scalar2=vcol[:, 16 + c8:17 + c8],
+                    op0=ALU.mult, op1=ALU.add,
+                )
+            else:
+                nc.scalar.activation(
+                    out=H_t[g][:, c8, :], in_=src, func=ACT.Identity,
+                    scale=g32[:, c8:c8 + 1], bias=vcol[:, 16 + c8:17 + c8],
+                )
+
+        def regroup(g, c):
+            if c == 0:
+                hg_t[g] = work.tile([P, 2, 2048], BF16, name="hg", tag="hg", align_bytes=64)
+            dst = hg_t[g][:, c, :].rearrange("p (m t) -> p m t", t=4).rearrange("p (c i) t -> p c t i", i=4)
+            src = H_t[g][:, 4 * c:4 * c + 4, :].rearrange("p t (c i) -> p c t i", i=4)
+            nc.vector.tensor_copy(out=dst, in_=src)
+
+        def hquant(g, c):
+            if c == 0:
+                h_codes[g] = work.tile([P, 2, 512], U32, name="hc", tag="hc", bufs=3, align_bytes=64)
+                h_scales[g] = work.tile([P, 2, 512], U8, name="hs", tag="hs", bufs=3, align_bytes=64)
+            nc.vector.quantize_mx(out=h_codes[g][:, c, :].bitcast(FP8X4), scales=h_scales[g][:, c, :], in_=hg_t[g][:, c, :])
+
+        ff_t = {}
+        sg_t = {}
+        s2_ps = {}
+
+        def s2_mm(n):
+            g, j = divmod(n, 4)
+            ps = psum.tile([P, 512], F32, name="s2_ps", tag="s2", bufs=2)
+            for c in range(2):
+                nc.tensor.matmul_mx(
+                    out=ps[:],
+                    lhsT=h_codes[g][:, c, j * P:(j + 1) * P].bitcast(FP8X4),
+                    lhsT_scale=h_scales[g][:, c, j * P:(j + 1) * P],
+                    rhs=w_codes[:, c, :].bitcast(FP8X4),
+                    rhs_scale=w_scales[:, c, :],
+                    start=(c == 0),
+                    stop=(c == 1),
+                )
+            s2_ps[n] = ps
+
+        def silu(n):
+            sg = work.tile([P, FF], F32, name="sg", tag="sg", bufs=3)
+            nc.scalar.activation(out=sg[:], in_=s2_ps[n][:, 0:FF], func=ACT.Silu)
+            sg_t[n] = sg
+
+        def ffmul(n):
+            g, j = divmod(n, 4)
+            if j == 0:
+                ff_t[g] = work.tile([P, 4, FF], F32, name="ff", tag="ff", bufs=2)
+            nc.vector.tensor_tensor(out=ff_t[g][:, j, :], in0=s2_ps[n][:, FF:2 * FF], in1=sg_t[n][:], op=ALU.mult)
+            if j == 3:
+                nc.sync.dma_start(out=o1_f[g * 512:(g + 1) * 512, :].rearrange("(p j) f -> p j f", j=4), in_=ff_t[g][:])
+
+        for q in range(2):
+            attn_q(q, attn_t(q))
+
+        vps = psum.tile([P, P], BF16, name="v_ps", tag="tp", bufs=3)
+        nc.tensor.transpose(vps[:], vec[:], ident_b[:])
+        nc.vector.tensor_copy(out=vcol[:], in_=vps[:, 0:24])
+        nc.vector.scalar_tensor_tensor(out=g32[:], in0=vcol[:, 0:8], scalar=32.0, in1=vcol[:, 8:16], op0=ALU.mult, op1=ALU.mult)
+
+        wg = {}
+
+        def w_prep(c, rp):
+            if c == 0 and rp == 0:
+                wg[0] = work.tile([P, 2, 2048], BF16, name="wg", tag="hg", align_bytes=64)
+            ps = psum.tile([P, 2, 4, P], BF16, name="w_ps", tag="tp", bufs=3)
+            for rr in range(2):
+                for t in range(4):
+                    k0 = (4 * c + t) * P
+                    nc.tensor.transpose(ps[:, rr, t, :], w_sb[:, 2 * rp + rr, k0:k0 + P], ident_b[:])
+            dst = wg[0][:, c, rp * 1024:(rp + 1) * 1024].rearrange("p (r f t) -> p r f t", r=2, t=4)
+            src = ps[:].rearrange("p r t f -> p r f t")
+            nc.scalar.copy(out=dst, in_=src)
+            if rp == 1:
+                nc.vector.quantize_mx(out=w_codes[:, c, :].bitcast(FP8X4), scales=w_scales[:, c, :], in_=wg[0][:, c, :])
+
+        pend_ag = {}
+        n_steps = NT + LS + 2
+        for n in range(n_steps):
+            if n >= 5 and (n - 5) % 4 == 0:
+                g = (n - 5) // 4 + XB
+                if g < NG:
+                    load(g)
+            tp_list = []
+            if n % 2 == 1:
+                q = (n + 3) // 2
+                if q < NT // 2:
+                    pend_ag[q] = attn_t(q)
+            if 1 <= n <= 4:
+                w_prep((n - 1) // 2, (n - 1) % 2)
+            gy, cp = divmod(n - LY, 4)
+            if 0 <= gy < NG:
+                for c8 in (2 * cp, 2 * cp + 1):
+                    tp_list.append((gy, c8, yt(gy, c8)))
+            pss = s1_mm(n) if n < NT else None
+            m = n - LS
+            if 0 <= m < NT:
+                s2_mm(m)
+            for (g_, c8, ps) in tp_list:
+                p4(g_, c8, ps)
+            if pss is not None:
+                p1(n, pss)
+            if 0 <= n - 1 < NT:
+                norm(n - 1)
+            if 0 <= m < NT:
+                silu(m)
+            gr, rr = divmod(n - LY - 2, 4)
+            if 0 <= gr < NG and rr in (0, 2):
+                regroup(gr, rr // 2)
+            if n % 2 == 1:
+                q = (n + 3) // 2
+                if q < NT // 2:
+                    attn_q(q, pend_ag[q])
+            if 0 <= m - 1 < NT:
+                ffmul(m - 1)
+            if 0 <= gr < NG and rr in (0, 2):
+                hquant(gr, rr // 2)

@@ -20,9 +20,10 @@ NT = NTOK // P
 NG = NT // 4
 FLOPS = 2 * NTOK * DA * D + 2 * NTOK * D * 2 * FF
 
-MANUAL = False
+MANUAL = True
 LY = 6
-LS = LY + 5
+LS = LY + 6
+P3B_V = False
 XB = 5
 P4_ON_V = ()
 ATCOPY_V = True
@@ -121,6 +122,9 @@ def tile_fractalblock_pb_t_kernel(tc, attn_out, x, o_w, norm2_w, scale_gamma, sc
                 for u in range(2):
                     c0 = (2 * pi + jj) * 256 + u * P
                     nc.tensor.transpose(ps[:, jj, u, :], af[:, c0:c0 + P], ident_f[:])
+            return ps
+
+        def attn_c(q, ps):
             ag = work.tile([P, 1024], BF16, name="ag", tag="ag", bufs=3, align_bytes=64)
             dst = ag[:].bitcast(F32).rearrange("p (t m u) -> p t m u", t=2, u=2)
             src = ps[:].rearrange("p t u m -> p t m u")
@@ -186,7 +190,10 @@ def tile_fractalblock_pb_t_kernel(tc, attn_out, x, o_w, norm2_w, scale_gamma, sc
             r = small.tile([P, 1], F32, name="r", tag="r")
             nc.gpsimd.tensor_tensor(out=r[:], in0=sse[:], in1=neg_half[:], op=ALU.pow)
             y = work.tile([P, D], F32, name="y", tag="y", bufs=12)
-            nc.gpsimd.tensor_scalar(out=y[:], in0=x1_t[q][:, jj, :], scalar1=r[:, 0:1], scalar2=0.0, op0=ALU.mult, op1=ALU.add)
+            if P3B_V:
+                nc.vector.tensor_scalar(out=y[:], in0=x1_t[q][:, jj, :], scalar1=r[:, 0:1], scalar2=None, op0=ALU.mult)
+            else:
+                nc.gpsimd.tensor_scalar(out=y[:], in0=x1_t[q][:, jj, :], scalar1=r[:, 0:1], scalar2=0.0, op0=ALU.mult, op1=ALU.add)
             y_t[n] = y
 
         H_t = {}
@@ -261,7 +268,7 @@ def tile_fractalblock_pb_t_kernel(tc, attn_out, x, o_w, norm2_w, scale_gamma, sc
                 nc.sync.dma_start(out=o1_f[g * 512:(g + 1) * 512, :].rearrange("(p j) f -> p j f", j=4), in_=ff_t[g][:])
 
         for q in range(2):
-            attn_q(q, attn_t(q))
+            attn_q(q, attn_c(q, attn_t(q)))
 
         vps = psum.tile([P, P], BF16, name="v_ps", tag="tp", bufs=3)
         nc.tensor.transpose(vps[:], vec[:], ident_b[:])
@@ -287,41 +294,38 @@ def tile_fractalblock_pb_t_kernel(tc, attn_out, x, o_w, norm2_w, scale_gamma, sc
         pend_ag = {}
         n_steps = NT + LS + 2
         for n in range(n_steps):
+            m = n - LS
             if n >= 5 and (n - 5) % 4 == 0:
                 g = (n - 5) // 4 + XB
                 if g < NG:
                     load(g)
-            tp_list = []
-            if n % 2 == 1:
-                q = (n + 3) // 2
-                if q < NT // 2:
-                    pend_ag[q] = attn_t(q)
-            if 1 <= n <= 4:
-                w_prep((n - 1) // 2, (n - 1) % 2)
-            gy, cp = divmod(n - LY, 4)
-            if 0 <= gy < NG:
-                for c8 in (2 * cp, 2 * cp + 1):
-                    tp_list.append((gy, c8, yt(gy, c8)))
-            pss = s1_mm(n) if n < NT else None
-            m = n - LS
-            if 0 <= m < NT:
-                s2_mm(m)
-            for (g_, c8, ps) in tp_list:
-                p4(g_, c8, ps)
-            if pss is not None:
-                p1(n, pss)
             if 0 <= n - 1 < NT:
                 norm(n - 1)
-            if 0 <= m < NT:
-                silu(m)
             gr, rr = divmod(n - LY - 2, 4)
             if 0 <= gr < NG and rr in (0, 2):
                 regroup(gr, rr // 2)
+            gq, rq = divmod(n - LY - 3, 4)
+            if 0 <= gq < NG and rq in (0, 2):
+                hquant(gq, rq // 2)
+            if n % 2 == 1:
+                q = (n + 1) // 2
+                if 2 <= q < NT // 2:
+                    attn_q(q, pend_ag[q])
+            gy, cp = divmod(n - LY, 4)
+            if 0 <= gy < NG:
+                p4(gy, 2 * cp, yt(gy, 2 * cp))
+            if n < NT:
+                p1(n, s1_mm(n))
+            if 0 <= gy < NG:
+                p4(gy, 2 * cp + 1, yt(gy, 2 * cp + 1))
+            if 1 <= n <= 4:
+                w_prep((n - 1) // 2, (n - 1) % 2)
             if n % 2 == 1:
                 q = (n + 3) // 2
                 if q < NT // 2:
-                    attn_q(q, pend_ag[q])
+                    pend_ag[q] = attn_c(q, attn_t(q))
+            if 0 <= m < NT:
+                s2_mm(m)
+                silu(m)
             if 0 <= m - 1 < NT:
                 ffmul(m - 1)
-            if 0 <= gr < NG and rr in (0, 2):
-                hquant(gr, rr // 2)

@@ -23,10 +23,10 @@ FLOPS = 2 * NTOK * DA * D + 2 * NTOK * D * 2 * FF
 MANUAL = True
 LY = 6
 LS = LY + 6
-P3B_V = False
+P3B_V = True
 XB = 5
 P4_ON_V = ()
-ATCOPY_V = True
+ATCOPY_V = False
 
 
 def tile_fractalblock_pb_t_kernel(tc, attn_out, x, o_w, norm2_w, scale_gamma, scale_beta, gate_w, up_w, out_0, out_1):
@@ -143,6 +143,7 @@ def tile_fractalblock_pb_t_kernel(tc, attn_out, x, o_w, norm2_w, scale_gamma, sc
 
         x1_t = {}
         y_t = {}
+        r_t = {}
 
         def s1_mm(n):
             q, jj = divmod(n, 2)
@@ -189,6 +190,11 @@ def tile_fractalblock_pb_t_kernel(tc, attn_out, x, o_w, norm2_w, scale_gamma, sc
             nc.gpsimd.tensor_scalar(out=sse[:], in0=ss[:], scalar1=1.0, scalar2=2.0 ** -13, op0=ALU.mult, op1=ALU.add)
             r = small.tile([P, 1], F32, name="r", tag="r")
             nc.gpsimd.tensor_tensor(out=r[:], in0=sse[:], in1=neg_half[:], op=ALU.pow)
+            r_t[n] = r
+
+        def scale_y(n):
+            q, jj = divmod(n, 2)
+            r = r_t[n]
             y = work.tile([P, D], F32, name="y", tag="y", bufs=12)
             if P3B_V:
                 nc.vector.tensor_scalar(out=y[:], in0=x1_t[q][:, jj, :], scalar1=r[:, 0:1], scalar2=None, op0=ALU.mult)
@@ -301,6 +307,8 @@ def tile_fractalblock_pb_t_kernel(tc, attn_out, x, o_w, norm2_w, scale_gamma, sc
                     load(g)
             if 0 <= n - 1 < NT:
                 norm(n - 1)
+            if 0 <= n - 2 < NT:
+                scale_y(n - 2)
             gr, rr = divmod(n - LY - 2, 4)
             if 0 <= gr < NG and rr in (0, 2):
                 regroup(gr, rr // 2)

@@ -20,10 +20,11 @@ NT = NTOK // P
 NG = NT // 4
 FLOPS = 2 * NTOK * DA * D + 2 * NTOK * D * 2 * FF
 
-MANUAL = True
+MANUAL = False
 LY = 6
 LS = LY + 6
 P3B_V = True
+TAIL_G = 1
 XB = 5
 P4_ON_V = ()
 ATCOPY_V = False
@@ -72,12 +73,18 @@ def tile_fractalblock_pb_t_kernel(tc, attn_out, x, o_w, norm2_w, scale_gamma, sc
             x_sb[g] = xx
 
         a0 = io.tile([P, 4 * DA], BF16, name="at_sb", tag="at_sb")
-        nc.sync.dma_start(out=a0[:], in_=attn_f[0:512, :].rearrange("(p j) k -> p (j k)", j=4))
-        at_sb[0] = a0
+        a0_src = attn_f[0:512, :].rearrange("(p j) k -> p (j k)", j=4)
         ow_sb = work.tile([P, 8, DA], BF16, name="ow_sb", tag="H")
-        nc.sync.dma_start(out=ow_sb[:], in_=o_w.rearrange("(t p) k -> p t k", p=P))
+        ow_src = o_w.rearrange("(t p) k -> p t k", p=P)
         x0 = io.tile([P, 4, D], BF16, name="x_sb", tag="x_sb")
-        nc.sync.dma_start(out=x0[:], in_=x_f[0:512, :].rearrange("(p j) d -> p j d", j=4))
+        x0_src = x_f[0:512, :].rearrange("(p j) d -> p j d", j=4)
+        nc.sync.dma_start(out=ow_sb[:, 0:4, :], in_=ow_src[:, 0:4, :])
+        nc.sync.dma_start(out=a0[:, 0:1024], in_=a0_src[:, 0:1024])
+        nc.sync.dma_start(out=ow_sb[:, 4:8, :], in_=ow_src[:, 4:8, :])
+        nc.sync.dma_start(out=x0[:, 0:2, :], in_=x0_src[:, 0:2, :])
+        nc.sync.dma_start(out=a0[:, 1024:2048], in_=a0_src[:, 1024:2048])
+        nc.sync.dma_start(out=x0[:, 2:4, :], in_=x0_src[:, 2:4, :])
+        at_sb[0] = a0
         x_sb[0] = x0
         nc.scalar.dma_start(out=vec[0:8, :], in_=norm2_w.rearrange("(c p) -> c p", p=P))
         nc.scalar.dma_start(out=vec[8:16, :], in_=scale_gamma.rearrange("(c p) -> c p", p=P))
@@ -217,7 +224,7 @@ def tile_fractalblock_pb_t_kernel(tc, attn_out, x, o_w, norm2_w, scale_gamma, sc
 
         def p4(g, c8, ps):
             src = ps[:].rearrange("p j m -> p (j m)")
-            if c8 in P4_ON_V:
+            if c8 in P4_ON_V or (g >= NG - TAIL_G and c8 % 2 == 1):
                 nc.vector.tensor_scalar(
                     out=H_t[g][:, c8, :], in0=src, scalar1=g32[:, c8:c8 + 1], scalar2=vcol[:, 16 + c8:17 + c8],
                     op0=ALU.mult, op1=ALU.add,
@@ -245,32 +252,36 @@ def tile_fractalblock_pb_t_kernel(tc, attn_out, x, o_w, norm2_w, scale_gamma, sc
         sg_t = {}
         s2_ps = {}
 
-        def s2_mm(n):
-            g, j = divmod(n, 4)
-            ps = psum.tile([P, 512], F32, name="s2_ps", tag="s2", bufs=2)
-            for c in range(2):
-                nc.tensor.matmul_mx(
-                    out=ps[:],
-                    lhsT=h_codes[g][:, c, j * P:(j + 1) * P].bitcast(FP8X4),
-                    lhsT_scale=h_scales[g][:, c, j * P:(j + 1) * P],
-                    rhs=w_codes[:, c, :].bitcast(FP8X4),
-                    rhs_scale=w_scales[:, c, :],
-                    start=(c == 0),
-                    stop=(c == 1),
-                )
-            s2_ps[n] = ps
+        def s2_mm(q):
+            g, pi = divmod(q, 2)
+            gate_ps = psum.tile([P, 2, FF], F32, name="gate_ps", tag="s2", bufs=2)
+            up_ps = psum.tile([P, 2, FF], F32, name="up_ps", tag="s2", bufs=2)
+            for jj in range(2):
+                j = 2 * pi + jj
+                for c in range(2):
+                    for (ps, w0) in ((gate_ps, 0), (up_ps, FF)):
+                        nc.tensor.matmul_mx(
+                            out=ps[:, jj, :],
+                            lhsT=h_codes[g][:, c, j * P:(j + 1) * P].bitcast(FP8X4),
+                            lhsT_scale=h_scales[g][:, c, j * P:(j + 1) * P],
+                            rhs=w_codes[:, c, w0:w0 + FF].bitcast(FP8X4),
+                            rhs_scale=w_scales[:, c, w0:w0 + FF],
+                            start=(c == 0),
+                            stop=(c == 1),
+                        )
+            s2_ps[q] = (gate_ps, up_ps)
 
-        def silu(n):
-            sg = work.tile([P, FF], F32, name="sg", tag="sg", bufs=3)
-            nc.scalar.activation(out=sg[:], in_=s2_ps[n][:, 0:FF], func=ACT.Silu)
-            sg_t[n] = sg
+        def silu(q):
+            sg = work.tile([P, 2, FF], F32, name="sg", tag="sg", bufs=2)
+            nc.scalar.activation(out=sg[:], in_=s2_ps[q][0][:], func=ACT.Silu)
+            sg_t[q] = sg
 
-        def ffmul(n):
-            g, j = divmod(n, 4)
-            if j == 0:
+        def ffmul(q):
+            g, pi = divmod(q, 2)
+            if pi == 0:
                 ff_t[g] = work.tile([P, 4, FF], F32, name="ff", tag="ff", bufs=2)
-            nc.vector.tensor_tensor(out=ff_t[g][:, j, :], in0=s2_ps[n][:, FF:2 * FF], in1=sg_t[n][:], op=ALU.mult)
-            if j == 3:
+            nc.vector.tensor_tensor(out=ff_t[g][:, 2 * pi:2 * pi + 2, :], in0=s2_ps[q][1][:], in1=sg_t[q][:], op=ALU.mult)
+            if pi == 1:
                 nc.sync.dma_start(out=o1_f[g * 512:(g + 1) * 512, :].rearrange("(p j) f -> p j f", j=4), in_=ff_t[g][:])
 
         for q in range(2):
@@ -332,8 +343,8 @@ def tile_fractalblock_pb_t_kernel(tc, attn_out, x, o_w, norm2_w, scale_gamma, sc
                 q = (n + 3) // 2
                 if q < NT // 2:
                     pend_ag[q] = attn_c(q, attn_t(q))
-            if 0 <= m < NT:
-                s2_mm(m)
-                silu(m)
-            if 0 <= m - 1 < NT:
-                ffmul(m - 1)
+            if 0 <= m < NT and m % 2 == 1:
+                s2_mm(m // 2)
+                silu(m // 2)
+            if 0 <= m - 1 < NT and (m - 1) % 2 == 1:
+                ffmul((m - 1) // 2)

@@ -24,7 +24,8 @@ MANUAL = False
 LY = 6
 LS = LY + 6
 P3B_V = True
-TAIL_G = 1
+TAIL_G = 0
+P3B_S_MOD = 4
 XB = 5
 P4_ON_V = ()
 ATCOPY_V = False
@@ -106,10 +107,7 @@ def tile_fractalblock_pb_t_kernel(tc, attn_out, x, o_w, norm2_w, scale_gamma, sc
                     nc.tensor.transpose(ps[:, tt, u, :], ow_f[:, c0:c0 + P], ident_f[:])
             dst = owg_f[:, b * 512:(b + 1) * 512].rearrange("p (t m u) -> p t m u", t=2, u=2)
             src = ps[:].rearrange("p t u m -> p t m u")
-            if b % 2 == 0:
-                nc.vector.tensor_copy(out=dst, in_=src)
-            else:
-                nc.scalar.copy(out=dst, in_=src)
+            nc.scalar.copy(out=dst, in_=src)
             if b % 2 == 1:
                 h = b // 2
                 nc.vector.quantize_mx(
@@ -203,7 +201,9 @@ def tile_fractalblock_pb_t_kernel(tc, attn_out, x, o_w, norm2_w, scale_gamma, sc
             q, jj = divmod(n, 2)
             r = r_t[n]
             y = work.tile([P, D], F32, name="y", tag="y", bufs=12)
-            if P3B_V:
+            if n % P3B_S_MOD == P3B_S_MOD - 1:
+                nc.scalar.activation(out=y[:], in_=x1_t[q][:, jj, :], func=ACT.Copy, scale=r[:, 0:1])
+            elif P3B_V:
                 nc.vector.tensor_scalar(out=y[:], in0=x1_t[q][:, jj, :], scalar1=r[:, 0:1], scalar2=None, op0=ALU.mult)
             else:
                 nc.gpsimd.tensor_scalar(out=y[:], in0=x1_t[q][:, jj, :], scalar1=r[:, 0:1], scalar2=0.0, op0=ALU.mult, op1=ALU.add)

@@ -20,15 +20,11 @@ NT = NTOK // P
 NG = NT // 4
 FLOPS = 2 * NTOK * DA * D + 2 * NTOK * D * 2 * FF
 
-MANUAL = False
 LY = 6
-LS = LY + 6
-P3B_V = True
-TAIL_G = 0
-P3B_S_MOD = 4
+DS = 5
+LAG = 3
 XB = 5
-P4_ON_V = ()
-ATCOPY_V = False
+W_STEPS = (4, 5, 6, 7)
 
 
 def tile_fractalblock_pb_t_kernel(tc, attn_out, x, o_w, norm2_w, scale_gamma, scale_beta, gate_w, up_w, out_0, out_1):
@@ -44,8 +40,7 @@ def tile_fractalblock_pb_t_kernel(tc, attn_out, x, o_w, norm2_w, scale_gamma, sc
         work = ctx.enter_context(tc.tile_pool(name="work", bufs=2))
         small = ctx.enter_context(tc.tile_pool(name="small", bufs=8))
         psum = ctx.enter_context(tc.psum_pool(name="psum", bufs=2))
-        if MANUAL:
-            ctx.enter_context(tc.manual_schedule())
+        ctx.enter_context(tc.manual_schedule())
 
         ident_f = const.tile([P, P], F32, name="ident_f")
         make_identity(nc, ident_f[:])
@@ -79,47 +74,29 @@ def tile_fractalblock_pb_t_kernel(tc, attn_out, x, o_w, norm2_w, scale_gamma, sc
         ow_src = o_w.rearrange("(t p) k -> p t k", p=P)
         x0 = io.tile([P, 4, D], BF16, name="x_sb", tag="x_sb")
         x0_src = x_f[0:512, :].rearrange("(p j) d -> p j d", j=4)
-        nc.sync.dma_start(out=ow_sb[:, 0:4, :], in_=ow_src[:, 0:4, :])
         nc.sync.dma_start(out=a0[:, 0:1024], in_=a0_src[:, 0:1024])
+        nc.sync.dma_start(out=ow_sb[:, 0:4, :], in_=ow_src[:, 0:4, :])
         nc.sync.dma_start(out=ow_sb[:, 4:8, :], in_=ow_src[:, 4:8, :])
-        nc.sync.dma_start(out=x0[:, 0:2, :], in_=x0_src[:, 0:2, :])
         nc.sync.dma_start(out=a0[:, 1024:2048], in_=a0_src[:, 1024:2048])
+        nc.sync.dma_start(out=x0[:, 0:2, :], in_=x0_src[:, 0:2, :])
         nc.sync.dma_start(out=x0[:, 2:4, :], in_=x0_src[:, 2:4, :])
         at_sb[0] = a0
         x_sb[0] = x0
         nc.scalar.dma_start(out=vec[0:8, :], in_=norm2_w.rearrange("(c p) -> c p", p=P))
         nc.scalar.dma_start(out=vec[8:16, :], in_=scale_gamma.rearrange("(c p) -> c p", p=P))
         nc.scalar.dma_start(out=vec[16:24, :], in_=scale_beta.rearrange("(c p) -> c p", p=P))
+        load(1)
         w_sb = work.tile([P, 4, D], BF16, name="w_sb", tag="H")
         nc.sync.dma_start(out=w_sb[:, 0:2, :], in_=gate_w.rearrange("(r p) k -> p r k", p=P))
         nc.sync.dma_start(out=w_sb[:, 2:4, :], in_=up_w.rearrange("(r p) k -> p r k", p=P))
-        for g in range(1, XB):
+        for g in range(2, XB):
             load(g)
-
-        owg = work.tile([P, 4 * D], BF16, name="owg", tag="hg", align_bytes=64)
-        owg_f = owg[:].bitcast(F32)
-        ow_f = ow_sb[:].rearrange("p t k -> p (t k)").bitcast(F32)
-        for b in range(4):
-            ps = psum.tile([P, 2, 2, P], F32, name="ow_ps", tag="tp", bufs=3)
-            for tt in range(2):
-                for u in range(2):
-                    c0 = (2 * b + tt) * 256 + u * P
-                    nc.tensor.transpose(ps[:, tt, u, :], ow_f[:, c0:c0 + P], ident_f[:])
-            dst = owg_f[:, b * 512:(b + 1) * 512].rearrange("p (t m u) -> p t m u", t=2, u=2)
-            src = ps[:].rearrange("p t u m -> p t m u")
-            nc.scalar.copy(out=dst, in_=src)
-            if b % 2 == 1:
-                h = b // 2
-                nc.vector.quantize_mx(
-                    out=ow_codes[:, h * 512:(h + 1) * 512].bitcast(FP8X4),
-                    scales=ow_scales[:, h * 512:(h + 1) * 512],
-                    in_=owg[:, h * 2048:(h + 1) * 2048],
-                )
 
         a_codes = {}
         a_scales = {}
+        ag_t = {}
 
-        def attn_t(q):
+        def attn_t(q, on_vector):
             g, pi = divmod(q, 2)
             af = at_sb[g][:].bitcast(F32)
             ps = psum.tile([P, 2, 2, P], F32, name="at_ps", tag="tp", bufs=3)
@@ -127,22 +104,19 @@ def tile_fractalblock_pb_t_kernel(tc, attn_out, x, o_w, norm2_w, scale_gamma, sc
                 for u in range(2):
                     c0 = (2 * pi + jj) * 256 + u * P
                     nc.tensor.transpose(ps[:, jj, u, :], af[:, c0:c0 + P], ident_f[:])
-            return ps
-
-        def attn_c(q, ps):
             ag = work.tile([P, 1024], BF16, name="ag", tag="ag", bufs=3, align_bytes=64)
             dst = ag[:].bitcast(F32).rearrange("p (t m u) -> p t m u", t=2, u=2)
             src = ps[:].rearrange("p t u m -> p t m u")
-            if ATCOPY_V:
+            if on_vector:
                 nc.vector.tensor_copy(out=dst, in_=src)
             else:
                 nc.scalar.copy(out=dst, in_=src)
-            return ag
+            ag_t[q] = ag
 
-        def attn_q(q, ag):
+        def attn_q(q):
             ac = work.tile([P, 256], U32, name="ac", tag="ac", bufs=4, align_bytes=64)
             asc = work.tile([P, 256], U8, name="asc", tag="asc", bufs=4, align_bytes=64)
-            nc.vector.quantize_mx(out=ac[:].bitcast(FP8X4), scales=asc[:], in_=ag[:])
+            nc.vector.quantize_mx(out=ac[:].bitcast(FP8X4), scales=asc[:], in_=ag_t[q][:])
             a_codes[q] = ac
             a_scales[q] = asc
 
@@ -150,9 +124,10 @@ def tile_fractalblock_pb_t_kernel(tc, attn_out, x, o_w, norm2_w, scale_gamma, sc
         y_t = {}
         r_t = {}
 
-        def s1_mm(n):
+        def s1(n):
             q, jj = divmod(n, 2)
-            outs = []
+            g, j = divmod(n, 4)
+            pss = []
             for hf in range(2):
                 ps = psum.tile([P, 512], F32, name="s1_ps", tag="s1", bufs=3)
                 nc.tensor.matmul_mx(
@@ -164,12 +139,7 @@ def tile_fractalblock_pb_t_kernel(tc, attn_out, x, o_w, norm2_w, scale_gamma, sc
                     start=True,
                     stop=True,
                 )
-                outs.append(ps)
-            return outs
-
-        def p1(n, pss):
-            q, jj = divmod(n, 2)
-            g, j = divmod(n, 4)
+                pss.append(ps)
             if jj == 0:
                 x1_t[q] = work.tile([P, 2, D], F32, name="x1", tag="x1", bufs=4)
             for hf in range(2):
@@ -199,14 +169,8 @@ def tile_fractalblock_pb_t_kernel(tc, attn_out, x, o_w, norm2_w, scale_gamma, sc
 
         def scale_y(n):
             q, jj = divmod(n, 2)
-            r = r_t[n]
-            y = work.tile([P, D], F32, name="y", tag="y", bufs=12)
-            if n % P3B_S_MOD == P3B_S_MOD - 1:
-                nc.scalar.activation(out=y[:], in_=x1_t[q][:, jj, :], func=ACT.Copy, scale=r[:, 0:1])
-            elif P3B_V:
-                nc.vector.tensor_scalar(out=y[:], in0=x1_t[q][:, jj, :], scalar1=r[:, 0:1], scalar2=None, op0=ALU.mult)
-            else:
-                nc.gpsimd.tensor_scalar(out=y[:], in0=x1_t[q][:, jj, :], scalar1=r[:, 0:1], scalar2=0.0, op0=ALU.mult, op1=ALU.add)
+            y = work.tile([P, D], F32, name="y", tag="y", bufs=10)
+            nc.vector.tensor_scalar(out=y[:], in0=x1_t[q][:, jj, :], scalar1=r_t[n][:, 0:1], scalar2=None, op0=ALU.mult)
             y_t[n] = y
 
         H_t = {}
@@ -220,42 +184,34 @@ def tile_fractalblock_pb_t_kernel(tc, attn_out, x, o_w, norm2_w, scale_gamma, sc
             ps = psum.tile([P, 4, P], F32, name="yt_ps", tag="tp", bufs=3)
             for j in range(4):
                 nc.tensor.transpose(ps[:, j, :], y_t[4 * g + j][:, c8 * P:(c8 + 1) * P], ident_f[:])
-            return ps
+            nc.scalar.activation(
+                out=H_t[g][:, c8, :], in_=ps[:].rearrange("p j m -> p (j m)"), func=ACT.Identity,
+                scale=g32[:, c8:c8 + 1], bias=vcol[:, 16 + c8:17 + c8],
+            )
 
-        def p4(g, c8, ps):
-            src = ps[:].rearrange("p j m -> p (j m)")
-            if c8 in P4_ON_V or (g >= NG - TAIL_G and c8 % 2 == 1):
-                nc.vector.tensor_scalar(
-                    out=H_t[g][:, c8, :], in0=src, scalar1=g32[:, c8:c8 + 1], scalar2=vcol[:, 16 + c8:17 + c8],
-                    op0=ALU.mult, op1=ALU.add,
-                )
-            else:
-                nc.scalar.activation(
-                    out=H_t[g][:, c8, :], in_=src, func=ACT.Identity,
-                    scale=g32[:, c8:c8 + 1], bias=vcol[:, 16 + c8:17 + c8],
-                )
-
-        def regroup(g, c):
+        def regroup(g, c, m0, m1):
             if c == 0:
                 hg_t[g] = work.tile([P, 2, 2048], BF16, name="hg", tag="hg", align_bytes=64)
-            dst = hg_t[g][:, c, :].rearrange("p (m t) -> p m t", t=4).rearrange("p (c i) t -> p c t i", i=4)
-            src = H_t[g][:, 4 * c:4 * c + 4, :].rearrange("p t (c i) -> p c t i", i=4)
+            dst = hg_t[g][:, c, 4 * m0:4 * m1].rearrange("p (m t) -> p m t", t=4).rearrange("p (c i) t -> p c t i", i=4)
+            src = H_t[g][:, 4 * c:4 * c + 4, m0:m1].rearrange("p t (c i) -> p c t i", i=4)
             nc.vector.tensor_copy(out=dst, in_=src)
 
-        def hquant(g, c):
+        def hquant(g, c, m0, m1):
             if c == 0:
                 h_codes[g] = work.tile([P, 2, 512], U32, name="hc", tag="hc", bufs=3, align_bytes=64)
                 h_scales[g] = work.tile([P, 2, 512], U8, name="hs", tag="hs", bufs=3, align_bytes=64)
-            nc.vector.quantize_mx(out=h_codes[g][:, c, :].bitcast(FP8X4), scales=h_scales[g][:, c, :], in_=hg_t[g][:, c, :])
+            nc.vector.quantize_mx(
+                out=h_codes[g][:, c, m0:m1].bitcast(FP8X4), scales=h_scales[g][:, c, m0:m1], in_=hg_t[g][:, c, 4 * m0:4 * m1]
+            )
 
         ff_t = {}
         sg_t = {}
-        s2_ps = {}
+        up_t = {}
 
-        def s2_mm(q):
+        def s2(q, tag, nbufs):
             g, pi = divmod(q, 2)
-            gate_ps = psum.tile([P, 2, FF], F32, name="gate_ps", tag="s2", bufs=2)
-            up_ps = psum.tile([P, 2, FF], F32, name="up_ps", tag="s2", bufs=2)
+            gate_ps = psum.tile([P, 2, FF], F32, name="gate_ps", tag=tag, bufs=nbufs)
+            up_ps = psum.tile([P, 2, FF], F32, name="up_ps", tag=tag, bufs=nbufs)
             for jj in range(2):
                 j = 2 * pi + jj
                 for c in range(2):
@@ -269,28 +225,21 @@ def tile_fractalblock_pb_t_kernel(tc, attn_out, x, o_w, norm2_w, scale_gamma, sc
                             start=(c == 0),
                             stop=(c == 1),
                         )
-            s2_ps[q] = (gate_ps, up_ps)
-
-        def silu(q):
             sg = work.tile([P, 2, FF], F32, name="sg", tag="sg", bufs=2)
-            nc.scalar.activation(out=sg[:], in_=s2_ps[q][0][:], func=ACT.Silu)
+            nc.scalar.activation(out=sg[:], in_=gate_ps[:], func=ACT.Silu)
             sg_t[q] = sg
+            up_t[q] = up_ps
 
-        def ffmul(q):
+        def ffmul(q, store_pair):
             g, pi = divmod(q, 2)
             if pi == 0:
                 ff_t[g] = work.tile([P, 4, FF], F32, name="ff", tag="ff", bufs=2)
-            nc.vector.tensor_tensor(out=ff_t[g][:, 2 * pi:2 * pi + 2, :], in0=s2_ps[q][1][:], in1=sg_t[q][:], op=ALU.mult)
-            if pi == 1:
-                nc.sync.dma_start(out=o1_f[g * 512:(g + 1) * 512, :].rearrange("(p j) f -> p j f", j=4), in_=ff_t[g][:])
-
-        for q in range(2):
-            attn_q(q, attn_c(q, attn_t(q)))
-
-        vps = psum.tile([P, P], BF16, name="v_ps", tag="tp", bufs=3)
-        nc.tensor.transpose(vps[:], vec[:], ident_b[:])
-        nc.vector.tensor_copy(out=vcol[:], in_=vps[:, 0:24])
-        nc.vector.scalar_tensor_tensor(out=g32[:], in0=vcol[:, 0:8], scalar=32.0, in1=vcol[:, 8:16], op0=ALU.mult, op1=ALU.mult)
+            nc.vector.tensor_tensor(out=ff_t[g][:, 2 * pi:2 * pi + 2, :], in0=up_t[q][:], in1=sg_t[q][:], op=ALU.mult)
+            dst = o1_f[g * 512:(g + 1) * 512, :].rearrange("(p j) f -> p j f", j=4)
+            if store_pair:
+                nc.sync.dma_start(out=dst[:, 2 * pi:2 * pi + 2, :], in_=ff_t[g][:, 2 * pi:2 * pi + 2, :])
+            elif pi == 1:
+                nc.sync.dma_start(out=dst, in_=ff_t[g][:])
 
         wg = {}
 
@@ -303,48 +252,76 @@ def tile_fractalblock_pb_t_kernel(tc, attn_out, x, o_w, norm2_w, scale_gamma, sc
                     k0 = (4 * c + t) * P
                     nc.tensor.transpose(ps[:, rr, t, :], w_sb[:, 2 * rp + rr, k0:k0 + P], ident_b[:])
             dst = wg[0][:, c, rp * 1024:(rp + 1) * 1024].rearrange("p (r f t) -> p r f t", r=2, t=4)
-            src = ps[:].rearrange("p r t f -> p r f t")
-            nc.scalar.copy(out=dst, in_=src)
-            if rp == 1:
-                nc.vector.quantize_mx(out=w_codes[:, c, :].bitcast(FP8X4), scales=w_scales[:, c, :], in_=wg[0][:, c, :])
+            nc.scalar.copy(out=dst, in_=ps[:].rearrange("p r t f -> p r f t"))
 
-        pend_ag = {}
-        n_steps = NT + LS + 2
-        for n in range(n_steps):
-            m = n - LS
-            if n >= 5 and (n - 5) % 4 == 0:
-                g = (n - 5) // 4 + XB
-                if g < NG:
-                    load(g)
-            if 0 <= n - 1 < NT:
-                norm(n - 1)
-            if 0 <= n - 2 < NT:
-                scale_y(n - 2)
-            gr, rr = divmod(n - LY - 2, 4)
-            if 0 <= gr < NG and rr in (0, 2):
-                regroup(gr, rr // 2)
-            gq, rq = divmod(n - LY - 3, 4)
-            if 0 <= gq < NG and rq in (0, 2):
-                hquant(gq, rq // 2)
-            if n % 2 == 1:
-                q = (n + 1) // 2
-                if 2 <= q < NT // 2:
-                    attn_q(q, pend_ag[q])
-            gy, cp = divmod(n - LY, 4)
-            if 0 <= gy < NG:
-                p4(gy, 2 * cp, yt(gy, 2 * cp))
-            if n < NT:
-                p1(n, s1_mm(n))
-            if 0 <= gy < NG:
-                p4(gy, 2 * cp + 1, yt(gy, 2 * cp + 1))
-            if 1 <= n <= 4:
-                w_prep((n - 1) // 2, (n - 1) % 2)
-            if n % 2 == 1:
-                q = (n + 3) // 2
-                if q < NT // 2:
-                    pend_ag[q] = attn_c(q, attn_t(q))
-            if 0 <= m < NT and m % 2 == 1:
-                s2_mm(m // 2)
-                silu(m // 2)
-            if 0 <= m - 1 < NT and (m - 1) % 2 == 1:
-                ffmul((m - 1) // 2)
+        def w_quant(c):
+            nc.vector.quantize_mx(out=w_codes[:, c, :].bitcast(FP8X4), scales=w_scales[:, c, :], in_=wg[0][:, c, :])
+
+        attn_t(0, True)
+        attn_q(0)
+        owg = work.tile([P, 4 * D], BF16, name="owg", tag="hg", align_bytes=64)
+        owg_f = owg[:].bitcast(F32)
+        ow_f = ow_sb[:].rearrange("p t k -> p (t k)").bitcast(F32)
+        for b in range(4):
+            ps = psum.tile([P, 2, 2, P], F32, name="ow_ps", tag="tp", bufs=3)
+            for tt in range(2):
+                for u in range(2):
+                    c0 = (2 * b + tt) * 256 + u * P
+                    nc.tensor.transpose(ps[:, tt, u, :], ow_f[:, c0:c0 + P], ident_f[:])
+            dst = owg_f[:, b * 512:(b + 1) * 512].rearrange("p (t m u) -> p t m u", t=2, u=2)
+            src = ps[:].rearrange("p t u m -> p t m u")
+            if b % 2 == 0:
+                nc.vector.tensor_copy(out=dst, in_=src)
+            else:
+                nc.scalar.copy(out=dst, in_=src)
+                h = b // 2
+                nc.vector.quantize_mx(
+                    out=ow_codes[:, h * 512:(h + 1) * 512].bitcast(FP8X4),
+                    scales=ow_scales[:, h * 512:(h + 1) * 512],
+                    in_=owg[:, h * 2048:(h + 1) * 2048],
+                )
+        attn_t(1, True)
+        attn_q(1)
+        vps = psum.tile([P, P], BF16, name="v_ps", tag="tp", bufs=3)
+        nc.tensor.transpose(vps[:], vec[:], ident_b[:])
+        nc.vector.tensor_copy(out=vcol[:], in_=vps[:, 0:24])
+        nc.vector.scalar_tensor_tensor(out=g32[:], in0=vcol[:, 0:8], scalar=32.0, in1=vcol[:, 8:16], op0=ALU.mult, op1=ALU.mult)
+
+        plan = []
+        for g in range(XB, NG):
+            plan.append((4 * (g - XB) + 5, 0, lambda g=g: load(g)))
+        for n in range(NT):
+            plan.append((n, 40, lambda n=n: s1(n)))
+            plan.append((n + 1, 10, lambda n=n: norm(n)))
+            plan.append((n + LAG, 20, lambda n=n: scale_y(n)))
+        for q in range(2, NT // 2):
+            plan.append((2 * q - 3, 60, lambda q=q: attn_t(q, False)))
+            plan.append((2 * q - 1, 23, lambda q=q: attn_q(q)))
+        for i in range(4):
+            plan.append((W_STEPS[i], 61, lambda i=i: w_prep(i // 2, i % 2)))
+            if i % 2 == 1:
+                plan.append((W_STEPS[i] + 1, 24, lambda i=i: w_quant(i // 2)))
+        for g in range(NG):
+            s0 = 4 * g + LY
+            last = g == NG - 1
+            for c8 in range(8):
+                plan.append((s0 + c8 // 2, 30 + 20 * (c8 % 2), lambda g=g, c8=c8: yt(g, c8)))
+            plan.append((s0 + 2, 21, lambda g=g: regroup(g, 0, 0, 512)))
+            plan.append((s0 + 3, 22, lambda g=g: hquant(g, 0, 0, 512)))
+            if not last:
+                plan.append((s0 + 4, 21, lambda g=g: regroup(g, 1, 0, 512)))
+                plan.append((s0 + 5, 22, lambda g=g: hquant(g, 1, 0, 512)))
+                for pi in range(2):
+                    plan.append((s0 + DS + 2 * pi, 70, lambda g=g, pi=pi: s2(2 * g + pi, "s2", 2)))
+                    plan.append((s0 + DS + 2 * pi + 1, 80, lambda g=g, pi=pi: ffmul(2 * g + pi, False)))
+            else:
+                plan.append((s0 + 4, 21, lambda g=g: regroup(g, 1, 0, 256)))
+                plan.append((s0 + 4, 22, lambda g=g: regroup(g, 1, 256, 512)))
+                plan.append((s0 + 4, 23, lambda g=g: hquant(g, 1, 0, 256)))
+                plan.append((s0 + 4, 24, lambda g=g: hquant(g, 1, 256, 512)))
+                plan.append((s0 + 4, 70, lambda g=g: s2(2 * g, "s2", 2)))
+                plan.append((s0 + 4, 71, lambda g=g: s2(2 * g + 1, "s1", 3)))
+                plan.append((s0 + 5, 80, lambda g=g: ffmul(2 * g, True)))
+                plan.append((s0 + 5, 81, lambda g=g: ffmul(2 * g + 1, True)))
+        for item in sorted(plan, key=lambda it: (it[0], it[1])):
+            item[2]()

@@ -208,27 +208,33 @@ def tile_fractalblock_pb_t_kernel(tc, attn_out, x, o_w, norm2_w, scale_gamma, sc
         sg_t = {}
         up_t = {}
 
-        def s2(q, tag, nbufs):
+        gate_t = {}
+
+        def s2_tile(q, jj, tag, nbufs):
             g, pi = divmod(q, 2)
-            gate_ps = psum.tile([P, 2, FF], F32, name="gate_ps", tag=tag, bufs=nbufs)
-            up_ps = psum.tile([P, 2, FF], F32, name="up_ps", tag=tag, bufs=nbufs)
-            for jj in range(2):
-                j = 2 * pi + jj
-                for c in range(2):
-                    for (ps, w0) in ((gate_ps, 0), (up_ps, FF)):
-                        nc.tensor.matmul_mx(
-                            out=ps[:, jj, :],
-                            lhsT=h_codes[g][:, c, j * P:(j + 1) * P].bitcast(FP8X4),
-                            lhsT_scale=h_scales[g][:, c, j * P:(j + 1) * P],
-                            rhs=w_codes[:, c, w0:w0 + FF].bitcast(FP8X4),
-                            rhs_scale=w_scales[:, c, w0:w0 + FF],
-                            start=(c == 0),
-                            stop=(c == 1),
-                        )
-            sg = work.tile([P, 2, FF], F32, name="sg", tag="sg", bufs=2)
-            nc.scalar.activation(out=sg[:], in_=gate_ps[:], func=ACT.Silu)
-            sg_t[q] = sg
-            up_t[q] = up_ps
+            if jj == 0:
+                gate_t[q] = psum.tile([P, 2, FF], F32, name="gate_ps", tag=tag, bufs=nbufs)
+                up_t[q] = psum.tile([P, 2, FF], F32, name="up_ps", tag=tag, bufs=nbufs)
+            j = 2 * pi + jj
+            for c in range(2):
+                for (ps, w0) in ((gate_t[q], 0), (up_t[q], FF)):
+                    nc.tensor.matmul_mx(
+                        out=ps[:, jj, :],
+                        lhsT=h_codes[g][:, c, j * P:(j + 1) * P].bitcast(FP8X4),
+                        lhsT_scale=h_scales[g][:, c, j * P:(j + 1) * P],
+                        rhs=w_codes[:, c, w0:w0 + FF].bitcast(FP8X4),
+                        rhs_scale=w_scales[:, c, w0:w0 + FF],
+                        start=(c == 0),
+                        stop=(c == 1),
+                    )
+            if jj == 1:
+                sg = work.tile([P, 2, FF], F32, name="sg", tag="sg", bufs=2)
+                nc.scalar.activation(out=sg[:], in_=gate_t[q][:], func=ACT.Silu)
+                sg_t[q] = sg
+
+        def s2(q, tag, nbufs):
+            s2_tile(q, 0, tag, nbufs)
+            s2_tile(q, 1, tag, nbufs)
 
         def ffmul(q, store_pair):
             g, pi = divmod(q, 2)
@@ -312,16 +318,17 @@ def tile_fractalblock_pb_t_kernel(tc, attn_out, x, o_w, norm2_w, scale_gamma, sc
                 plan.append((s0 + 4, 21, lambda g=g: regroup(g, 1, 0, 512)))
                 plan.append((s0 + 5, 22, lambda g=g: hquant(g, 1, 0, 512)))
                 for pi in range(2):
-                    plan.append((s0 + DS + 2 * pi, 70, lambda g=g, pi=pi: s2(2 * g + pi, "s2", 2)))
-                    plan.append((s0 + DS + 2 * pi + 1, 80, lambda g=g, pi=pi: ffmul(2 * g + pi, False)))
+                    plan.append((s0 + DS + 2 * pi, 70, lambda g=g, pi=pi: s2_tile(2 * g + pi, 0, "s2", 2)))
+                    plan.append((s0 + DS + 2 * pi + 1, 70, lambda g=g, pi=pi: s2_tile(2 * g + pi, 1, "s2", 2)))
+                    plan.append((s0 + DS + 2 * pi + 2, 80, lambda g=g, pi=pi: ffmul(2 * g + pi, False)))
             else:
                 plan.append((s0 + 4, 21, lambda g=g: regroup(g, 1, 0, 256)))
                 plan.append((s0 + 4, 22, lambda g=g: regroup(g, 1, 256, 512)))
                 plan.append((s0 + 4, 23, lambda g=g: hquant(g, 1, 0, 256)))
                 plan.append((s0 + 4, 24, lambda g=g: hquant(g, 1, 256, 512)))
-                plan.append((s0 + 4, 70, lambda g=g: s2(2 * g, "s2", 2)))
-                plan.append((s0 + 4, 71, lambda g=g: s2(2 * g + 1, "s1", 3)))
-                plan.append((s0 + 5, 80, lambda g=g: ffmul(2 * g, True)))
-                plan.append((s0 + 5, 81, lambda g=g: ffmul(2 * g + 1, True)))
+                plan.append((s0 + 4, 71, lambda g=g: s2(2 * g, "s1", 3)))
+                plan.append((s0 + 4, 72, lambda g=g: s2(2 * g + 1, "tp", 3)))
+                plan.append((s0 + 5, 81, lambda g=g: ffmul(2 * g, True)))
+                plan.append((s0 + 5, 82, lambda g=g: ffmul(2 * g + 1, True)))
         for item in sorted(plan, key=lambda it: (it[0], it[1])):
             item[2]()

from contextlib import ExitStack

import concourse.mybir as mybir
from concourse.masks import make_identity

F32 = mybir.dt.float32
BF16 = mybir.dt.bfloat16
U32 = mybir.dt.uint32
U8 = mybir.dt.uint8
FP8X4 = mybir.dt.float8_e4m3fn_x4
ALU = mybir.AluOpType
ACT = mybir.ActivationFunctionType

P = 128
NTOK = 4096
DA = 512
D = 1024
FF = 256
NT = NTOK // P
NG = NT // 4
FLOPS = 2 * NTOK * DA * D + 2 * NTOK * D * 2 * FF

LY = 6
DS = 5
LAG = 3
XB = 5
W_STEPS = (4, 5, 6, 7)


def tile_fractalblock_pb_t_kernel(tc, attn_out, x, o_w, norm2_w, scale_gamma, scale_beta, gate_w, up_w, out_0, out_1):
    nc = tc.nc
    attn_f = attn_out.flatten_outer_dims()
    x_f = x.flatten_outer_dims()
    o0_f = out_0.flatten_outer_dims()
    o1_f = out_1.flatten_outer_dims()

    with ExitStack() as ctx:
        const = ctx.enter_context(tc.tile_pool(name="const", bufs=1))
        io = ctx.enter_context(tc.tile_pool(name="io", bufs=XB))
        work = ctx.enter_context(tc.tile_pool(name="work", bufs=2))
        small = ctx.enter_context(tc.tile_pool(name="small", bufs=8))
        psum = ctx.enter_context(tc.psum_pool(name="psum", bufs=2))
        ctx.enter_context(tc.manual_schedule())

        ident_f = const.tile([P, P], F32, name="ident_f")
        make_identity(nc, ident_f[:])
        ident_b = const.tile([P, P], BF16, name="ident_b")
        make_identity(nc, ident_b[:])
        neg_half = const.tile([P, 1], F32, name="neg_half")
        nc.vector.memset(neg_half[:], -0.5)
        vec = const.tile([P, P], BF16, name="vec")
        nc.vector.memset(vec[:], 0.0)
        vcol = const.tile([P, 24], F32, name="vcol")
        g32 = const.tile([P, 8], F32, name="g32")
        ow_codes = const.tile([P, D], U32, name="ow_codes", align_bytes=64)
        ow_scales = const.tile([P, D], U8, name="ow_scales", align_bytes=64)
        w_codes = const.tile([P, 2, 512], U32, name="w_codes", align_bytes=64)
        w_scales = const.tile([P, 2, 512], U8, name="w_scales", align_bytes=64)

        x_sb = {}
        at_sb = {}

        def load(g):
            a = io.tile([P, 4 * DA], BF16, name="at_sb", tag="at_sb")
            nc.sync.dma_start(out=a[:], in_=attn_f[g * 512:(g + 1) * 512, :].rearrange("(p j) k -> p (j k)", j=4))
            at_sb[g] = a
            xx = io.tile([P, 4, D], BF16, name="x_sb", tag="x_sb")
            nc.sync.dma_start(out=xx[:], in_=x_f[g * 512:(g + 1) * 512, :].rearrange("(p j) d -> p j d", j=4))
            x_sb[g] = xx

        a0 = io.tile([P, 4 * DA], BF16, name="at_sb", tag="at_sb")
        a0_src = attn_f[0:512, :].rearrange("(p j) k -> p (j k)", j=4)
        ow_sb = work.tile([P, 8, DA], BF16, name="ow_sb", tag="H")
        ow_src = o_w.rearrange("(t p) k -> p t k", p=P)
        x0 = io.tile([P, 4, D], BF16, name="x_sb", tag="x_sb")
        x0_src = x_f[0:512, :].rearrange("(p j) d -> p j d", j=4)
        nc.sync.dma_start(out=a0[:, 0:1024], in_=a0_src[:, 0:1024])
        nc.sync.dma_start(out=ow_sb[:, 0:4, :], in_=ow_src[:, 0:4, :])
        nc.sync.dma_start(out=ow_sb[:, 4:8, :], in_=ow_src[:, 4:8, :])
        nc.sync.dma_start(out=a0[:, 1024:2048], in_=a0_src[:, 1024:2048])
        nc.sync.dma_start(out=x0[:, 0:2, :], in_=x0_src[:, 0:2, :])
        nc.sync.dma_start(out=x0[:, 2:4, :], in_=x0_src[:, 2:4, :])
        at_sb[0] = a0
        x_sb[0] = x0
        nc.scalar.dma_start(out=vec[0:8, :], in_=norm2_w.rearrange("(c p) -> c p", p=P))
        nc.scalar.dma_start(out=vec[8:16, :], in_=scale_gamma.rearrange("(c p) -> c p", p=P))
        nc.scalar.dma_start(out=vec[16:24, :], in_=scale_beta.rearrange("(c p) -> c p", p=P))
        load(1)
        w_sb = work.tile([P, 4, D], BF16, name="w_sb", tag="H")
        nc.sync.dma_start(out=w_sb[:, 0:2, :], in_=gate_w.rearrange("(r p) k -> p r k", p=P))
        nc.sync.dma_start(out=w_sb[:, 2:4, :], in_=up_w.rearrange("(r p) k -> p r k", p=P))
        for g in range(2, XB):
            load(g)

        a_codes = {}
        a_scales = {}
        ag_t = {}

        def attn_t(q, on_vector):
            g, pi = divmod(q, 2)
            af = at_sb[g][:].bitcast(F32)
            ps = psum.tile([P, 2, 2, P], F32, name="at_ps", tag="tp", bufs=3)
            for jj in range(2):
                for u in range(2):
                    c0 = (2 * pi + jj) * 256 + u * P
                    nc.tensor.transpose(ps[:, jj, u, :], af[:, c0:c0 + P], ident_f[:])
            ag = work.tile([P, 1024], BF16, name="ag", tag="ag", bufs=3, align_bytes=64)
            dst = ag[:].bitcast(F32).rearrange("p (t m u) -> p t m u", t=2, u=2)
            src = ps[:].rearrange("p t u m -> p t m u")
            if on_vector:
                nc.vector.tensor_copy(out=dst, in_=src)
            else:
                nc.scalar.copy(out=dst, in_=src)
            ag_t[q] = ag

        def attn_q(q):
            ac = work.tile([P, 256], U32, name="ac", tag="ac", bufs=4, align_bytes=64)
            asc = work.tile([P, 256], U8, name="asc", tag="asc", bufs=4, align_bytes=64)
            nc.vector.quantize_mx(out=ac[:].bitcast(FP8X4), scales=asc[:], in_=ag_t[q][:])
            a_codes[q] = ac
            a_scales[q] = asc

        x1_t = {}
        y_t = {}
        r_t = {}

        def s1(n):
            q, jj = divmod(n, 2)
            g, j = divmod(n, 4)
            pss = []
            for hf in range(2):
                ps = psum.tile([P, 512], F32, name="s1_ps", tag="s1", bufs=3)
                nc.tensor.matmul_mx(
                    out=ps[:],
                    lhsT=a_codes[q][:, jj * P:(jj + 1) * P].bitcast(FP8X4),
                    lhsT_scale=a_scales[q][:, jj * P:(jj + 1) * P],
                    rhs=ow_codes[:, hf * 512:(hf + 1) * 512].bitcast(FP8X4),
                    rhs_scale=ow_scales[:, hf * 512:(hf + 1) * 512],
                    start=True,
                    stop=True,
                )
                pss.append(ps)
            if jj == 0:
                x1_t[q] = work.tile([P, 2, D], F32, name="x1", tag="x1", bufs=4)
            for hf in range(2):
                nc.vector.tensor_tensor(
                    out=x1_t[q][:, jj, hf * 512:(hf + 1) * 512],
                    in0=pss[hf][:],
                    in1=x_sb[g][:, j, hf * 512:(hf + 1) * 512],
                    op=ALU.add,
                )
            if jj == 1:
                pi = q % 2
                nc.sync.dma_start(
                    out=o0_f[g * 512:(g + 1) * 512, :].rearrange("(p j) d -> p j d", j=4)[:, 2 * pi:2 * pi + 2, :],
                    in_=x1_t[q][:],
                )

        def norm(n):
            q, jj = divmod(n, 2)
            junk = work.tile([P, D], BF16, name="junk", tag="junk", bufs=2)
            ss = small.tile([P, 1], F32, name="ss", tag="ss")
            nc.scalar.activation(out=junk[:], in_=x1_t[q][:, jj, :], func=ACT.Square, accum_out=ss[:])
            sse = small.tile([P, 1], F32, name="sse", tag="sse")
            nc.gpsimd.tensor_scalar(out=sse[:], in0=ss[:], scalar1=1.0, scalar2=2.0 ** -13, op0=ALU.mult, op1=ALU.add)
            r = small.tile([P, 1], F32, name="r", tag="r")
            nc.gpsimd.tensor_tensor(out=r[:], in0=sse[:], in1=neg_half[:], op=ALU.pow)
            r_t[n] = r

        def scale_y(n):
            q, jj = divmod(n, 2)
            y = work.tile([P, D], F32, name="y", tag="y", bufs=10)
            nc.vector.tensor_scalar(out=y[:], in0=x1_t[q][:, jj, :], scalar1=r_t[n][:, 0:1], scalar2=None, op0=ALU.mult)
            y_t[n] = y

        H_t = {}
        hg_t = {}
        h_codes = {}
        h_scales = {}

        def yt(g, c8):
            if c8 == 0:
                H_t[g] = work.tile([P, 8, 512], BF16, name="H", tag="H")
            ps = psum.tile([P, 4, P], F32, name="yt_ps", tag="tp", bufs=3)
            for j in range(4):
                nc.tensor.transpose(ps[:, j, :], y_t[4 * g + j][:, c8 * P:(c8 + 1) * P], ident_f[:])
            nc.scalar.activation(
                out=H_t[g][:, c8, :], in_=ps[:].rearrange("p j m -> p (j m)"), func=ACT.Identity,
                scale=g32[:, c8:c8 + 1], bias=vcol[:, 16 + c8:17 + c8],
            )

        def regroup(g, c, m0, m1):
            if c == 0:
                hg_t[g] = work.tile([P, 2, 2048], BF16, name="hg", tag="hg", align_bytes=64)
            dst = hg_t[g][:, c, 4 * m0:4 * m1].rearrange("p (m t) -> p m t", t=4).rearrange("p (c i) t -> p c t i", i=4)
            src = H_t[g][:, 4 * c:4 * c + 4, m0:m1].rearrange("p t (c i) -> p c t i", i=4)
            nc.vector.tensor_copy(out=dst, in_=src)

        def hquant(g, c, m0, m1):
            if c == 0:
                h_codes[g] = work.tile([P, 2, 512], U32, name="hc", tag="hc", bufs=3, align_bytes=64)
                h_scales[g] = work.tile([P, 2, 512], U8, name="hs", tag="hs", bufs=3, align_bytes=64)
            nc.vector.quantize_mx(
                out=h_codes[g][:, c, m0:m1].bitcast(FP8X4), scales=h_scales[g][:, c, m0:m1], in_=hg_t[g][:, c, 4 * m0:4 * m1]
            )

        ff_t = {}
        sg_t = {}
        up_t = {}

        gate_t = {}

        def s2_tile(q, jj, tag, nbufs):
            g, pi = divmod(q, 2)
            if jj == 0:
                gate_t[q] = psum.tile([P, 2, FF], F32, name="gate_ps", tag=tag, bufs=nbufs)
                up_t[q] = psum.tile([P, 2, FF], F32, name="up_ps", tag=tag, bufs=nbufs)
            j = 2 * pi + jj
            for c in range(2):
                for (ps, w0) in ((gate_t[q], 0), (up_t[q], FF)):
                    nc.tensor.matmul_mx(
                        out=ps[:, jj, :],
                        lhsT=h_codes[g][:, c, j * P:(j + 1) * P].bitcast(FP8X4),
                        lhsT_scale=h_scales[g][:, c, j * P:(j + 1) * P],
                        rhs=w_codes[:, c, w0:w0 + FF].bitcast(FP8X4),
                        rhs_scale=w_scales[:, c, w0:w0 + FF],
                        start=(c == 0),
                        stop=(c == 1),
                    )
            if jj == 1:
                sg = work.tile([P, 2, FF], F32, name="sg", tag="sg", bufs=2)
                nc.scalar.activation(out=sg[:], in_=gate_t[q][:], func=ACT.Silu)
                sg_t[q] = sg

        def s2(q, tag, nbufs):
            s2_tile(q, 0, tag, nbufs)
            s2_tile(q, 1, tag, nbufs)

        def ffmul(q, store_pair):
            g, pi = divmod(q, 2)
            if pi == 0:
                ff_t[g] = work.tile([P, 4, FF], F32, name="ff", tag="ff", bufs=2)
            nc.vector.tensor_tensor(out=ff_t[g][:, 2 * pi:2 * pi + 2, :], in0=up_t[q][:], in1=sg_t[q][:], op=ALU.mult)
            dst = o1_f[g * 512:(g + 1) * 512, :].rearrange("(p j) f -> p j f", j=4)
            if store_pair:
                nc.sync.dma_start(out=dst[:, 2 * pi:2 * pi + 2, :], in_=ff_t[g][:, 2 * pi:2 * pi + 2, :])
            elif pi == 1:
                nc.sync.dma_start(out=dst, in_=ff_t[g][:])

        wg = {}

        def w_prep(c, rp):
            if c == 0 and rp == 0:
                wg[0] = work.tile([P, 2, 2048], BF16, name="wg", tag="hg", align_bytes=64)
            ps = psum.tile([P, 2, 4, P], BF16, name="w_ps", tag="tp", bufs=3)
            for rr in range(2):
                for t in range(4):
                    k0 = (4 * c + t) * P
                    nc.tensor.transpose(ps[:, rr, t, :], w_sb[:, 2 * rp + rr, k0:k0 + P], ident_b[:])
            dst = wg[0][:, c, rp * 1024:(rp + 1) * 1024].rearrange("p (r f t) -> p r f t", r=2, t=4)
            nc.scalar.copy(out=dst, in_=ps[:].rearrange("p r t f -> p r f t"))

        def w_quant(c):
            nc.vector.quantize_mx(out=w_codes[:, c, :].bitcast(FP8X4), scales=w_scales[:, c, :], in_=wg[0][:, c, :])

        attn_t(0, True)
        attn_q(0)
        owg = work.tile([P, 4 * D], BF16, name="owg", tag="hg", align_bytes=64)
        owg_f = owg[:].bitcast(F32)
        ow_f = ow_sb[:].rearrange("p t k -> p (t k)").bitcast(F32)
        for b in range(4):
            ps = psum.tile([P, 2, 2, P], F32, name="ow_ps", tag="tp", bufs=3)
            for tt in range(2):
                for u in range(2):
                    c0 = (2 * b + tt) * 256 + u * P
                    nc.tensor.transpose(ps[:, tt, u, :], ow_f[:, c0:c0 + P], ident_f[:])
            dst = owg_f[:, b * 512:(b + 1) * 512].rearrange("p (t m u) -> p t m u", t=2, u=2)
            src = ps[:].rearrange("p t u m -> p t m u")
            if b % 2 == 0:
                nc.vector.tensor_copy(out=dst, in_=src)
            else:
                nc.scalar.copy(out=dst, in_=src)
                h = b // 2
                nc.vector.quantize_mx(
                    out=ow_codes[:, h * 512:(h + 1) * 512].bitcast(FP8X4),
                    scales=ow_scales[:, h * 512:(h + 1) * 512],
                    in_=owg[:, h * 2048:(h + 1) * 2048],
                )
        attn_t(1, True)
        attn_q(1)
        vps = psum.tile([P, P], BF16, name="v_ps", tag="tp", bufs=3)
        nc.tensor.transpose(vps[:], vec[:], ident_b[:])
        nc.vector.tensor_copy(out=vcol[:], in_=vps[:, 0:24])
        nc.vector.scalar_tensor_tensor(out=g32[:], in0=vcol[:, 0:8], scalar=32.0, in1=vcol[:, 8:16], op0=ALU.mult, op1=ALU.mult)

        plan = []
        for g in range(XB, NG):
            plan.append((4 * (g - XB) + 5, 0, lambda g=g: load(g)))
        for n in range(NT):
            plan.append((n, 40, lambda n=n: s1(n)))
            plan.append((n + 1, 10, lambda n=n: norm(n)))
            plan.append((n + LAG, 20, lambda n=n: scale_y(n)))
        for q in range(2, NT // 2):
            plan.append((2 * q - 3, 60, lambda q=q: attn_t(q, False)))
            plan.append((2 * q - 1, 23, lambda q=q: attn_q(q)))
        for i in range(4):
            plan.append((W_STEPS[i], 61, lambda i=i: w_prep(i // 2, i % 2)))
            if i % 2 == 1:
                plan.append((W_STEPS[i] + 1, 24, lambda i=i: w_quant(i // 2)))
        for g in range(NG):
            s0 = 4 * g + LY
            last = g == NG - 1
            for c8 in range(8):
                plan.append((s0 + c8 // 2, 30 + 20 * (c8 % 2), lambda g=g, c8=c8: yt(g, c8)))
            plan.append((s0 + 2, 21, lambda g=g: regroup(g, 0, 0, 512)))
            plan.append((s0 + 3, 22, lambda g=g: hquant(g, 0, 0, 512)))
            if not last:
                plan.append((s0 + 4, 21, lambda g=g: regroup(g, 1, 0, 512)))
                plan.append((s0 + 5, 22, lambda g=g: hquant(g, 1, 0, 512)))
                for pi in range(2):
                    plan.append((s0 + DS + 2 * pi, 70, lambda g=g, pi=pi: s2_tile(2 * g + pi, 0, "s2", 2)))
                    plan.append((s0 + DS + 2 * pi + 1, 70, lambda g=g, pi=pi: s2_tile(2 * g + pi, 1, "s2", 2)))
                    plan.append((s0 + DS + 2 * pi + 2, 80, lambda g=g, pi=pi: ffmul(2 * g + pi, False)))
            else:
                plan.append((s0 + 4, 21, lambda g=g: regroup(g, 1, 0, 256)))
                plan.append((s0 + 4, 22, lambda g=g: regroup(g, 1, 256, 512)))
                plan.append((s0 + 4, 23, lambda g=g: hquant(g, 1, 0, 256)))
                plan.append((s0 + 4, 24, lambda g=g: hquant(g, 1, 256, 512)))
                plan.append((s0 + 4, 71, lambda g=g: s2(2 * g, "s1", 3)))
                plan.append((s0 + 4, 72, lambda g=g: s2(2 * g + 1, "tp", 3)))
                plan.append((s0 + 5, 81, lambda g=g: ffmul(2 * g, True)))
                plan.append((s0 + 5, 82, lambda g=g: ffmul(2 * g + 1, True)))
        for item in sorted(plan, key=lambda it: (it[0], it[1])):
            item[2]()
